import numpy as np
import ml_dtypes

BF16 = ml_dtypes.bfloat16


def bf(x):
    return np.asarray(x, np.float32).astype(BF16)


def f32(x):
    return np.asarray(x, np.float32)


def f64(x):
    return np.asarray(x).astype(np.float64)


def striped(idx):
    return np.tile(idx.reshape(-1, 16).T, (8, 1))


C, S, N, N0, N1, R, M0, M1 = 256, 512, 256, 2, 128, 128, 128, 2
ALPHA = 1.5


def setup_inputs():
    return {
        "x": bf(np.random.standard_normal((N0, N1, C))),
        "core1": bf(np.random.uniform(-0.1, 0.1, (N1, M1, R))),
        "core0": bf(np.random.uniform(-0.1, 0.1, (N0, R, M0))),
        "scale": f32(1.0 + 0.1 * np.random.standard_normal((1, N))),
        "bias": f32(0.1 * np.random.standard_normal((1, N))),
        "base": f32(np.random.standard_normal((C, S))),
        "offs": striped(np.random.permutation(S)[:N]),
    }


def reference(x, core1, core0, scale, bias, base, offs):
    idx = offs[:16].T.reshape(-1)
    t = np.einsum("pkc,kmr->pmrc", f64(x), f64(core1))
    y = np.einsum("pmrc,pri->cmi", t, f64(core0)).reshape(C, N)
    out = f64(base).copy()
    out[:, idx] = y * (ALPHA * f64(scale)) + f64(bias)
    return out

@@ -1,0 +1,74 @@
+import concourse.mybir as mybir
+
+BF16, F32, U16 = mybir.dt.bfloat16, mybir.dt.float32, mybir.dt.uint16
+MULT, ADD = mybir.AluOpType.mult, mybir.AluOpType.add
+COPY = mybir.ActivationFunctionType.Copy
+
+P = 128
+C, S, N = 256, 512, 256
+N0, N1 = 2, 128
+M1, M0 = 2, 128
+R = 128
+ALPHA = 1.5
+TOKEN_BLOCKS = C // P
+
+FLOPS = 2 * (N0 * M1 * R * C) * N1 + 2 * (C * M1 * M0) * (N0 * R)
+
+
+def tile_tensorizedlinear_kernel(tc, x, core1, core0, scale, bias, base, offs, out):
+    nc = tc.nc
+    with (
+        tc.tile_pool(name="held", bufs=1) as held,
+        tc.tile_pool(name="work", bufs=2) as work,
+        tc.psum_pool(name="psum", bufs=2) as psum,
+    ):
+        x_sb = held.tile([P, N0, C], BF16, name="x_sb")
+        nc.sync.dma_start(x_sb[:], x.rearrange("p k c -> k p c"))
+        core1_sb = held.tile([P, M1, R], BF16, name="core1_sb")
+        nc.scalar.dma_start(core1_sb[:], core1)
+        core0_sb = held.tile([P, N0, M0], BF16, name="core0_sb")
+        nc.scalar.dma_start(core0_sb[:], core0.rearrange("p r i -> r p i"))
+        offsets = held.tile([P, N // 16], U16, name="offsets")
+        nc.sync.dma_start(offsets[:], offs)
+
+        scale_all = held.tile([P, N], F32, name="scale_all")
+        nc.gpsimd.dma_start(scale_all[:], scale.rearrange("o n -> (o n)").partition_broadcast(P))
+        bias_all = held.tile([P, N], F32, name="bias_all")
+        nc.gpsimd.dma_start(bias_all[:], bias.rearrange("o n -> (o n)").partition_broadcast(P))
+
+        windows = [held.tile([P, S], F32, name=f"window{b}") for b in range(TOKEN_BLOCKS)]
+        nc.sync.dma_start(windows[0][:], base[0:P, :])
+        nc.scalar.dma_start(windows[1][:], base[P : 2 * P, :])
+
+        gain_all = held.tile([P, N], F32, name="gain_all")
+        nc.gpsimd.tensor_scalar_mul(gain_all[:], scale_all[:], ALPHA)
+
+        for b in range(TOKEN_BLOCKS):
+            tokens = slice(b * P, (b + 1) * P)
+
+            t_sb = []
+            for m in range(M1):
+                t_ps = psum.tile([P, N0, P], F32, name=f"t_ps{m}")
+                nc.tensor.matmul(t_ps[:], core1_sb[:, m, :], x_sb[:, :, tokens], start=True, stop=True)
+                t_m = work.tile([P, N0, P], BF16, name=f"t_sb{m}")
+                if m == 0:
+                    nc.vector.tensor_copy(t_m[:], t_ps[:])
+                else:
+                    nc.scalar.activation(t_m[:], t_ps[:], COPY)
+                t_sb.append(t_m)
+
+            y_ps = psum.tile([P, N], F32, name="y_ps")
+            for m in range(M1):
+                for p in range(N0):
+                    nc.tensor.matmul(
+                        y_ps[:, m * M0 : (m + 1) * M0],
+                        t_sb[m][:, p, :],
+                        core0_sb[:, p, :],
+                        start=(p == 0),
+                        stop=(p == N0 - 1),
+                    )
+
+            y_gained = work.tile([P, N], F32, name="y_gained")
+            nc.vector.tensor_tensor(y_gained[:], y_ps[:], gain_all[:], MULT)
+            nc.vector.tensor_tensor(windows[b][:].indirect(offsets[:]), y_gained[:], bias_all[:], ADD)
+            nc.sync.dma_start(out[tokens, :], windows[b][:])

@@ -32,9 +32,9 @@ def tile_tensorizedlinear_kernel(tc, x, core1, core0, scale, bias, base, offs, o
         nc.sync.dma_start(offsets[:], offs)
 
         scale_all = held.tile([P, N], F32, name="scale_all")
-        nc.gpsimd.dma_start(scale_all[:], scale.rearrange("o n -> (o n)").partition_broadcast(P))
+        nc.sync.dma_start(scale_all[:], scale.rearrange("o n -> (o n)").partition_broadcast(P))
         bias_all = held.tile([P, N], F32, name="bias_all")
-        nc.gpsimd.dma_start(bias_all[:], bias.rearrange("o n -> (o n)").partition_broadcast(P))
+        nc.scalar.dma_start(bias_all[:], bias.rearrange("o n -> (o n)").partition_broadcast(P))
 
         windows = [held.tile([P, S], F32, name=f"window{b}") for b in range(TOKEN_BLOCKS)]
         nc.sync.dma_start(windows[0][:], base[0:P, :])

@@ -23,25 +23,22 @@ def tile_tensorizedlinear_kernel(tc, x, core1, core0, scale, bias, base, offs, o
         tc.psum_pool(name="psum", bufs=2) as psum,
     ):
         x_sb = held.tile([P, N0, C], BF16, name="x_sb")
-        nc.sync.dma_start(x_sb[:], x.rearrange("p k c -> k p c"))
         core1_sb = held.tile([P, M1, R], BF16, name="core1_sb")
-        nc.scalar.dma_start(core1_sb[:], core1)
         core0_sb = held.tile([P, N0, M0], BF16, name="core0_sb")
-        nc.scalar.dma_start(core0_sb[:], core0.rearrange("p r i -> r p i"))
-        offsets = held.tile([P, N // 16], U16, name="offsets")
-        nc.sync.dma_start(offsets[:], offs)
-
         scale_all = held.tile([P, N], F32, name="scale_all")
-        nc.sync.dma_start(scale_all[:], scale.rearrange("o n -> (o n)").partition_broadcast(P))
         bias_all = held.tile([P, N], F32, name="bias_all")
-        nc.scalar.dma_start(bias_all[:], bias.rearrange("o n -> (o n)").partition_broadcast(P))
-
-        windows = [held.tile([P, S], F32, name=f"window{b}") for b in range(TOKEN_BLOCKS)]
-        nc.sync.dma_start(windows[0][:], base[0:P, :])
-        nc.scalar.dma_start(windows[1][:], base[P : 2 * P, :])
-
         gain_all = held.tile([P, N], F32, name="gain_all")
-        nc.gpsimd.tensor_scalar_mul(gain_all[:], scale_all[:], ALPHA)
+        offsets = held.tile([P, N // 16], U16, name="offsets")
+        windows = [held.tile([P, S], F32, name=f"window{b}") for b in range(TOKEN_BLOCKS)]
+
+        nc.sync.dma_start(x_sb[:], x.rearrange("p k c -> k p c"))
+        nc.scalar.dma_start(core1_sb[:], core1)
+        nc.gpsimd.dma_start(windows[1][:], base[P : 2 * P, :])
+        nc.scalar.dma_start(core0_sb[:], core0.rearrange("p r i -> r p i"))
+        nc.sync.dma_start(scale_all[:], scale.rearrange("o n -> (o n)").partition_broadcast(P))
+        nc.sync.dma_start(windows[0][:], base[0:P, :])
+        nc.scalar.dma_start(bias_all[:], bias.rearrange("o n -> (o n)").partition_broadcast(P))
+        nc.sync.dma_start(offsets[:], offs)
 
         for b in range(TOKEN_BLOCKS):
             tokens = slice(b * P, (b + 1) * P)
@@ -51,11 +48,14 @@ def tile_tensorizedlinear_kernel(tc, x, core1, core0, scale, bias, base, offs, o
                 t_ps = psum.tile([P, N0, P], F32, name=f"t_ps{m}")
                 nc.tensor.matmul(t_ps[:], core1_sb[:, m, :], x_sb[:, :, tokens], start=True, stop=True)
                 t_m = work.tile([P, N0, P], BF16, name=f"t_sb{m}")
-                if m == 0:
+                if b == 0 and m == 0:
                     nc.vector.tensor_copy(t_m[:], t_ps[:])
                 else:
                     nc.scalar.activation(t_m[:], t_ps[:], COPY)
                 t_sb.append(t_m)
+
+            if b == 0:
+                nc.vector.tensor_scalar_mul(gain_all[:], scale_all[:], ALPHA)
 
             y_ps = psum.tile([P, N], F32, name="y_ps")
             for m in range(M1):

@@ -33,19 +33,19 @@ def tile_tensorizedlinear_kernel(tc, x, core1, core0, scale, bias, base, offs, o
 
         nc.sync.dma_start(x_sb[:], x.rearrange("p k c -> k p c"))
         nc.scalar.dma_start(core1_sb[:], core1)
-        nc.gpsimd.dma_start(windows[1][:], base[P : 2 * P, :])
-        nc.scalar.dma_start(core0_sb[:], core0.rearrange("p r i -> r p i"))
-        nc.sync.dma_start(scale_all[:], scale.rearrange("o n -> (o n)").partition_broadcast(P))
+        nc.sync.dma_start(core0_sb[:], core0.rearrange("p r i -> r p i"))
+        nc.scalar.dma_start(scale_all[:], scale.rearrange("o n -> (o n)").partition_broadcast(P))
         nc.sync.dma_start(windows[0][:], base[0:P, :])
-        nc.scalar.dma_start(bias_all[:], bias.rearrange("o n -> (o n)").partition_broadcast(P))
         nc.sync.dma_start(offsets[:], offs)
+        nc.sync.dma_start(bias_all[:], bias.rearrange("o n -> (o n)").partition_broadcast(P))
+        nc.sync.dma_start(windows[1][:], base[P : 2 * P, :])
 
         for b in range(TOKEN_BLOCKS):
             tokens = slice(b * P, (b + 1) * P)
 
             t_sb = []
             for m in range(M1):
-                t_ps = psum.tile([P, N0, P], F32, name=f"t_ps{m}")
+                t_ps = psum.tile([P, N0, P], BF16, name=f"t_ps{m}")
                 nc.tensor.matmul(t_ps[:], core1_sb[:, m, :], x_sb[:, :, tokens], start=True, stop=True)
                 t_m = work.tile([P, N0, P], BF16, name=f"t_sb{m}")
                 if b == 0 and m == 0:

@@ -17,17 +17,19 @@ FLOPS = 2 * (N0 * M1 * R * C) * N1 + 2 * (C * M1 * M0) * (N0 * R)
 
 def tile_tensorizedlinear_kernel(tc, x, core1, core0, scale, bias, base, offs, out):
     nc = tc.nc
+    pieces = M1 * N0
     with (
         tc.tile_pool(name="held", bufs=1) as held,
-        tc.tile_pool(name="work", bufs=2) as work,
-        tc.psum_pool(name="psum", bufs=2) as psum,
+        tc.tile_pool(name="t_pool", bufs=TOKEN_BLOCKS * pieces) as t_pool,
+        tc.tile_pool(name="y_pool", bufs=TOKEN_BLOCKS) as y_pool,
+        tc.psum_pool(name="t_psum", bufs=pieces) as t_psum,
+        tc.psum_pool(name="y_psum", bufs=TOKEN_BLOCKS * M1) as y_psum,
     ):
         x_sb = held.tile([P, N0, C], BF16, name="x_sb")
         core1_sb = held.tile([P, M1, R], BF16, name="core1_sb")
         core0_sb = held.tile([P, N0, M0], BF16, name="core0_sb")
         scale_all = held.tile([P, N], F32, name="scale_all")
         bias_all = held.tile([P, N], F32, name="bias_all")
-        gain_all = held.tile([P, N], F32, name="gain_all")
         offsets = held.tile([P, N // 16], U16, name="offsets")
         windows = [held.tile([P, S], F32, name=f"window{b}") for b in range(TOKEN_BLOCKS)]
 
@@ -43,32 +45,29 @@ def tile_tensorizedlinear_kernel(tc, x, core1, core0, scale, bias, base, offs, o
         for b in range(TOKEN_BLOCKS):
             tokens = slice(b * P, (b + 1) * P)
 
-            t_sb = []
-            for m in range(M1):
-                t_ps = psum.tile([P, N0, P], BF16, name=f"t_ps{m}")
-                nc.tensor.matmul(t_ps[:], core1_sb[:, m, :], x_sb[:, :, tokens], start=True, stop=True)
-                t_m = work.tile([P, N0, P], BF16, name=f"t_sb{m}")
-                if b == 0 and m == 0:
-                    nc.vector.tensor_copy(t_m[:], t_ps[:])
-                else:
-                    nc.scalar.activation(t_m[:], t_ps[:], COPY)
-                t_sb.append(t_m)
-
-            if b == 0:
-                nc.vector.tensor_scalar_mul(gain_all[:], scale_all[:], ALPHA)
-
-            y_ps = psum.tile([P, N], F32, name="y_ps")
+            t_sb = {}
             for m in range(M1):
                 for p in range(N0):
-                    nc.tensor.matmul(
-                        y_ps[:, m * M0 : (m + 1) * M0],
-                        t_sb[m][:, p, :],
-                        core0_sb[:, p, :],
-                        start=(p == 0),
-                        stop=(p == N0 - 1),
-                    )
+                    t_ps = t_psum.tile([P, P], BF16, name="t_ps")
+                    nc.tensor.matmul(t_ps[:], core1_sb[:, m, :], x_sb[:, p, tokens], start=True, stop=True)
+                    t_piece = t_pool.tile([P, P], BF16, name="t_piece")
+                    if b == 0:
+                        nc.vector.tensor_copy(t_piece[:], t_ps[:])
+                    else:
+                        nc.scalar.activation(t_piece[:], t_ps[:], COPY)
+                    t_sb[m, p] = t_piece
 
-            y_gained = work.tile([P, N], F32, name="y_gained")
-            nc.vector.tensor_tensor(y_gained[:], y_ps[:], gain_all[:], MULT)
-            nc.vector.tensor_tensor(windows[b][:].indirect(offsets[:]), y_gained[:], bias_all[:], ADD)
+            y_scaled = y_pool.tile([P, N], F32, name="y_scaled")
+            for m in range(M1):
+                features = slice(m * M0, (m + 1) * M0)
+                y_ps = y_psum.tile([P, M0], F32, name="y_ps")
+                for p in range(N0):
+                    nc.tensor.matmul(
+                        y_ps[:], t_sb[m, p][:], core0_sb[:, p, :], start=(p == 0), stop=(p == N0 - 1)
+                    )
+                nc.vector.scalar_tensor_tensor(
+                    y_scaled[:, features], y_ps[:], ALPHA, scale_all[:, features], MULT, MULT
+                )
+
+            nc.vector.tensor_tensor(windows[b][:].indirect(offsets[:]), y_scaled[:], bias_all[:], ADD)
             nc.sync.dma_start(out[tokens, :], windows[b][:])

@@ -2,7 +2,6 @@ import concourse.mybir as mybir
 
 BF16, F32, U16 = mybir.dt.bfloat16, mybir.dt.float32, mybir.dt.uint16
 MULT, ADD = mybir.AluOpType.mult, mybir.AluOpType.add
-COPY = mybir.ActivationFunctionType.Copy
 
 P = 128
 C, S, N = 256, 512, 256
@@ -42,32 +41,30 @@ def tile_tensorizedlinear_kernel(tc, x, core1, core0, scale, bias, base, offs, o
         nc.sync.dma_start(bias_all[:], bias.rearrange("o n -> (o n)").partition_broadcast(P))
         nc.sync.dma_start(windows[1][:], base[P : 2 * P, :])
 
+        t_sb = {}
         for b in range(TOKEN_BLOCKS):
-            tokens = slice(b * P, (b + 1) * P)
-
-            t_sb = {}
             for m in range(M1):
                 for p in range(N0):
                     t_ps = t_psum.tile([P, P], BF16, name="t_ps")
-                    nc.tensor.matmul(t_ps[:], core1_sb[:, m, :], x_sb[:, p, tokens], start=True, stop=True)
+                    nc.tensor.matmul(
+                        t_ps[:], core1_sb[:, m, :], x_sb[:, p, b * P : (b + 1) * P], start=True, stop=True
+                    )
                     t_piece = t_pool.tile([P, P], BF16, name="t_piece")
-                    if b == 0:
-                        nc.vector.tensor_copy(t_piece[:], t_ps[:])
-                    else:
-                        nc.scalar.activation(t_piece[:], t_ps[:], COPY)
-                    t_sb[m, p] = t_piece
+                    nc.vector.tensor_copy(t_piece[:], t_ps[:])
+                    t_sb[b, m, p] = t_piece
 
+        for b in range(TOKEN_BLOCKS):
             y_scaled = y_pool.tile([P, N], F32, name="y_scaled")
             for m in range(M1):
                 features = slice(m * M0, (m + 1) * M0)
                 y_ps = y_psum.tile([P, M0], F32, name="y_ps")
                 for p in range(N0):
                     nc.tensor.matmul(
-                        y_ps[:], t_sb[m, p][:], core0_sb[:, p, :], start=(p == 0), stop=(p == N0 - 1)
+                        y_ps[:], t_sb[b, m, p][:], core0_sb[:, p, :], start=(p == 0), stop=(p == N0 - 1)
                     )
                 nc.vector.scalar_tensor_tensor(
                     y_scaled[:, features], y_ps[:], ALPHA, scale_all[:, features], MULT, MULT
                 )
 
             nc.vector.tensor_tensor(windows[b][:].indirect(offsets[:]), y_scaled[:], bias_all[:], ADD)
-            nc.sync.dma_start(out[tokens, :], windows[b][:])
+            nc.sync.dma_start(out[b * P : (b + 1) * P, :], windows[b][:])

@@ -16,12 +16,12 @@ FLOPS = 2 * (N0 * M1 * R * C) * N1 + 2 * (C * M1 * M0) * (N0 * R)
 
 def tile_tensorizedlinear_kernel(tc, x, core1, core0, scale, bias, base, offs, out):
     nc = tc.nc
-    pieces = M1 * N0
+    pieces = M1
     with (
         tc.tile_pool(name="held", bufs=1) as held,
         tc.tile_pool(name="t_pool", bufs=TOKEN_BLOCKS * pieces) as t_pool,
         tc.tile_pool(name="y_pool", bufs=TOKEN_BLOCKS) as y_pool,
-        tc.psum_pool(name="t_psum", bufs=pieces) as t_psum,
+        tc.psum_pool(name="t_psum", bufs=TOKEN_BLOCKS * pieces) as t_psum,
         tc.psum_pool(name="y_psum", bufs=TOKEN_BLOCKS * M1) as y_psum,
     ):
         x_sb = held.tile([P, N0, C], BF16, name="x_sb")
@@ -41,30 +41,28 @@ def tile_tensorizedlinear_kernel(tc, x, core1, core0, scale, bias, base, offs, o
         nc.sync.dma_start(bias_all[:], bias.rearrange("o n -> (o n)").partition_broadcast(P))
         nc.sync.dma_start(windows[1][:], base[P : 2 * P, :])
 
-        t_sb = {}
         for b in range(TOKEN_BLOCKS):
-            for m in range(M1):
-                for p in range(N0):
-                    t_ps = t_psum.tile([P, P], BF16, name="t_ps")
-                    nc.tensor.matmul(
-                        t_ps[:], core1_sb[:, m, :], x_sb[:, p, b * P : (b + 1) * P], start=True, stop=True
-                    )
-                    t_piece = t_pool.tile([P, P], BF16, name="t_piece")
-                    nc.vector.tensor_copy(t_piece[:], t_ps[:])
-                    t_sb[b, m, p] = t_piece
+            tokens = slice(b * P, (b + 1) * P)
 
-        for b in range(TOKEN_BLOCKS):
+            t_sb = []
+            for m in range(M1):
+                t_ps = t_psum.tile([P, N0, P], BF16, name="t_ps")
+                nc.tensor.matmul(t_ps[:], core1_sb[:, m, :], x_sb[:, :, tokens], start=True, stop=True)
+                t_piece = t_pool.tile([P, N0, P], BF16, name="t_piece")
+                nc.vector.tensor_copy(t_piece[:], t_ps[:])
+                t_sb.append(t_piece)
+
             y_scaled = y_pool.tile([P, N], F32, name="y_scaled")
             for m in range(M1):
                 features = slice(m * M0, (m + 1) * M0)
                 y_ps = y_psum.tile([P, M0], F32, name="y_ps")
                 for p in range(N0):
                     nc.tensor.matmul(
-                        y_ps[:], t_sb[b, m, p][:], core0_sb[:, p, :], start=(p == 0), stop=(p == N0 - 1)
+                        y_ps[:], t_sb[m][:, p, :], core0_sb[:, p, :], start=(p == 0), stop=(p == N0 - 1)
                     )
                 nc.vector.scalar_tensor_tensor(
                     y_scaled[:, features], y_ps[:], ALPHA, scale_all[:, features], MULT, MULT
                 )
 
             nc.vector.tensor_tensor(windows[b][:].indirect(offsets[:]), y_scaled[:], bias_all[:], ADD)
-            nc.sync.dma_start(out[b * P : (b + 1) * P, :], windows[b][:])
+            nc.sync.dma_start(out[tokens, :], windows[b][:])

@@ -10,6 +10,7 @@ M1, M0 = 2, 128
 R = 128
 ALPHA = 1.5
 TOKEN_BLOCKS = C // P
+B = 32
 
 FLOPS = 2 * (N0 * M1 * R * C) * N1 + 2 * (C * M1 * M0) * (N0 * R)
 
@@ -27,19 +28,33 @@ def tile_tensorizedlinear_kernel(tc, x, core1, core0, scale, bias, base, offs, o
         x_sb = held.tile([P, N0, C], BF16, name="x_sb")
         core1_sb = held.tile([P, M1, R], BF16, name="core1_sb")
         core0_sb = held.tile([P, N0, M0], BF16, name="core0_sb")
-        scale_all = held.tile([P, N], F32, name="scale_all")
-        bias_all = held.tile([P, N], F32, name="bias_all")
         offsets = held.tile([P, N // 16], U16, name="offsets")
         windows = [held.tile([P, S], F32, name=f"window{b}") for b in range(TOKEN_BLOCKS)]
 
         nc.sync.dma_start(x_sb[:], x.rearrange("p k c -> k p c"))
         nc.scalar.dma_start(core1_sb[:], core1)
         nc.sync.dma_start(core0_sb[:], core0.rearrange("p r i -> r p i"))
-        nc.scalar.dma_start(scale_all[:], scale.rearrange("o n -> (o n)").partition_broadcast(P))
+        rows = [held.tile([P, N], F32, name=f"rows{v}", align_bytes=64) for v in range(2)]
+        for v, vector in enumerate((scale, bias)):
+            nc.vector.memset(rows[v][:], 0.0)
+            nc.scalar.dma_start(rows[v][::B, :], vector.rearrange("o n -> (o n)").partition_broadcast(P // B))
         nc.sync.dma_start(windows[0][:], base[0:P, :])
         nc.sync.dma_start(offsets[:], offs)
-        nc.sync.dma_start(bias_all[:], bias.rearrange("o n -> (o n)").partition_broadcast(P))
         nc.sync.dma_start(windows[1][:], base[P : 2 * P, :])
+
+        spread_rows = []
+        for v in range(2):
+            column = held.tile([P, N], F32, name=f"column{v}", align_bytes=64)
+            nc.vector.transpose(column[:], rows[v][:])
+            repeated = held.tile([P, N], F32, name=f"repeated{v}", align_bytes=64)
+            nc.vector.tensor_copy(
+                repeated[:].rearrange("p (b i) -> p b i", i=B),
+                column[:].rearrange("p (b i) -> p b i", i=B)[:, :, 0:1].to_broadcast([P, N // B, B]),
+            )
+            spread = held.tile([P, N], F32, name=f"spread{v}", align_bytes=64)
+            nc.vector.transpose(spread[:], repeated[:])
+            spread_rows.append(spread)
+        scale_all, bias_all = spread_rows
 
         for b in range(TOKEN_BLOCKS):
             tokens = slice(b * P, (b + 1) * P)

@@ -33,23 +33,23 @@ def tile_tensorizedlinear_kernel(tc, x, core1, core0, scale, bias, base, offs, o
 
         nc.sync.dma_start(x_sb[:], x.rearrange("p k c -> k p c"))
         nc.scalar.dma_start(core1_sb[:], core1)
-        nc.sync.dma_start(core0_sb[:], core0.rearrange("p r i -> r p i"))
-        rows = [held.tile([P, N], F32, name=f"rows{v}", align_bytes=64) for v in range(2)]
+        nc.scalar.dma_start(core0_sb[:], core0.rearrange("p r i -> r p i"))
+        rows = held.tile([P, N], F32, name="rows", align_bytes=64)
+        nc.gpsimd.memset(rows[:], 0.0)
         for v, vector in enumerate((scale, bias)):
-            nc.vector.memset(rows[v][:], 0.0)
-            nc.scalar.dma_start(rows[v][::B, :], vector.rearrange("o n -> (o n)").partition_broadcast(P // B))
+            nc.sync.dma_start(rows[v::B, :], vector.rearrange("o n -> (o n)").partition_broadcast(P // B))
         nc.sync.dma_start(windows[0][:], base[0:P, :])
         nc.sync.dma_start(offsets[:], offs)
         nc.sync.dma_start(windows[1][:], base[P : 2 * P, :])
 
+        columns = held.tile([P, N], F32, name="columns", align_bytes=64)
+        nc.vector.transpose(columns[:], rows[:])
         spread_rows = []
         for v in range(2):
-            column = held.tile([P, N], F32, name=f"column{v}", align_bytes=64)
-            nc.vector.transpose(column[:], rows[v][:])
             repeated = held.tile([P, N], F32, name=f"repeated{v}", align_bytes=64)
             nc.vector.tensor_copy(
                 repeated[:].rearrange("p (b i) -> p b i", i=B),
-                column[:].rearrange("p (b i) -> p b i", i=B)[:, :, 0:1].to_broadcast([P, N // B, B]),
+                columns[:].rearrange("p (b i) -> p b i", i=B)[:, :, v : v + 1].to_broadcast([P, N // B, B]),
             )
             spread = held.tile([P, N], F32, name=f"spread{v}", align_bytes=64)
             nc.vector.transpose(spread[:], repeated[:])
@@ -64,7 +64,7 @@ def tile_tensorizedlinear_kernel(tc, x, core1, core0, scale, bias, base, offs, o
                 t_ps = t_psum.tile([P, N0, P], BF16, name="t_ps")
                 nc.tensor.matmul(t_ps[:], core1_sb[:, m, :], x_sb[:, :, tokens], start=True, stop=True)
                 t_piece = t_pool.tile([P, N0, P], BF16, name="t_piece")
-                nc.vector.tensor_copy(t_piece[:], t_ps[:])
+                nc.scalar.copy(t_piece[:], t_ps[:])
                 t_sb.append(t_piece)
 
             y_scaled = y_pool.tile([P, N], F32, name="y_scaled")

@@ -21,7 +21,7 @@ def tile_tensorizedlinear_kernel(tc, x, core1, core0, scale, bias, base, offs, o
     with (
         tc.tile_pool(name="held", bufs=1) as held,
         tc.tile_pool(name="t_pool", bufs=TOKEN_BLOCKS * pieces) as t_pool,
-        tc.tile_pool(name="y_pool", bufs=TOKEN_BLOCKS) as y_pool,
+        tc.tile_pool(name="y_pool", bufs=1) as y_pool,
         tc.psum_pool(name="t_psum", bufs=TOKEN_BLOCKS * pieces) as t_psum,
         tc.psum_pool(name="y_psum", bufs=TOKEN_BLOCKS * M1) as y_psum,
     ):
@@ -33,11 +33,11 @@ def tile_tensorizedlinear_kernel(tc, x, core1, core0, scale, bias, base, offs, o
 
         nc.sync.dma_start(x_sb[:], x.rearrange("p k c -> k p c"))
         nc.scalar.dma_start(core1_sb[:], core1)
-        nc.scalar.dma_start(core0_sb[:], core0.rearrange("p r i -> r p i"))
         rows = held.tile([P, N], F32, name="rows", align_bytes=64)
         nc.gpsimd.memset(rows[:], 0.0)
         for v, vector in enumerate((scale, bias)):
             nc.sync.dma_start(rows[v::B, :], vector.rearrange("o n -> (o n)").partition_broadcast(P // B))
+        nc.sync.dma_start(core0_sb[:], core0.rearrange("p r i -> r p i"))
         nc.sync.dma_start(windows[0][:], base[0:P, :])
         nc.sync.dma_start(offsets[:], offs)
         nc.sync.dma_start(windows[1][:], base[P : 2 * P, :])
@@ -56,28 +56,30 @@ def tile_tensorizedlinear_kernel(tc, x, core1, core0, scale, bias, base, offs, o
             spread_rows.append(spread)
         scale_all, bias_all = spread_rows
 
-        for b in range(TOKEN_BLOCKS):
-            tokens = slice(b * P, (b + 1) * P)
-
-            t_sb = []
-            for m in range(M1):
+        t_sb = {}
+        for m in range(M1):
+            for b in range(TOKEN_BLOCKS):
                 t_ps = t_psum.tile([P, N0, P], BF16, name="t_ps")
-                nc.tensor.matmul(t_ps[:], core1_sb[:, m, :], x_sb[:, :, tokens], start=True, stop=True)
+                nc.tensor.matmul(
+                    t_ps[:], core1_sb[:, m, :], x_sb[:, :, b * P : (b + 1) * P], start=True, stop=True
+                )
                 t_piece = t_pool.tile([P, N0, P], BF16, name="t_piece")
                 nc.scalar.copy(t_piece[:], t_ps[:])
-                t_sb.append(t_piece)
+                t_sb[b, m] = t_piece
 
-            y_scaled = y_pool.tile([P, N], F32, name="y_scaled")
-            for m in range(M1):
-                features = slice(m * M0, (m + 1) * M0)
+        y_scaled = [y_pool.tile([P, N], F32, name=f"y_scaled{b}") for b in range(TOKEN_BLOCKS)]
+        for m in range(M1):
+            features = slice(m * M0, (m + 1) * M0)
+            for b in range(TOKEN_BLOCKS):
                 y_ps = y_psum.tile([P, M0], F32, name="y_ps")
                 for p in range(N0):
                     nc.tensor.matmul(
-                        y_ps[:], t_sb[m][:, p, :], core0_sb[:, p, :], start=(p == 0), stop=(p == N0 - 1)
+                        y_ps[:], t_sb[b, m][:, p, :], core0_sb[:, p, :], start=(p == 0), stop=(p == N0 - 1)
                     )
                 nc.vector.scalar_tensor_tensor(
-                    y_scaled[:, features], y_ps[:], ALPHA, scale_all[:, features], MULT, MULT
+                    y_scaled[b][:, features], y_ps[:], ALPHA, scale_all[:, features], MULT, MULT
                 )
 
-            nc.vector.tensor_tensor(windows[b][:].indirect(offsets[:]), y_scaled[:], bias_all[:], ADD)
-            nc.sync.dma_start(out[tokens, :], windows[b][:])
+        for b in range(TOKEN_BLOCKS):
+            nc.vector.tensor_tensor(windows[b][:].indirect(offsets[:]), y_scaled[b][:], bias_all[:], ADD)
+            nc.sync.dma_start(out[b * P : (b + 1) * P, :], windows[b][:])

@@ -33,11 +33,11 @@ def tile_tensorizedlinear_kernel(tc, x, core1, core0, scale, bias, base, offs, o
 
         nc.sync.dma_start(x_sb[:], x.rearrange("p k c -> k p c"))
         nc.scalar.dma_start(core1_sb[:], core1)
+        nc.scalar.dma_start(core0_sb[:], core0.rearrange("p r i -> r p i"))
         rows = held.tile([P, N], F32, name="rows", align_bytes=64)
         nc.gpsimd.memset(rows[:], 0.0)
         for v, vector in enumerate((scale, bias)):
             nc.sync.dma_start(rows[v::B, :], vector.rearrange("o n -> (o n)").partition_broadcast(P // B))
-        nc.sync.dma_start(core0_sb[:], core0.rearrange("p r i -> r p i"))
         nc.sync.dma_start(windows[0][:], base[0:P, :])
         nc.sync.dma_start(offsets[:], offs)
         nc.sync.dma_start(windows[1][:], base[P : 2 * P, :])

@@ -35,7 +35,7 @@ def tile_tensorizedlinear_kernel(tc, x, core1, core0, scale, bias, base, offs, o
         nc.scalar.dma_start(core1_sb[:], core1)
         nc.scalar.dma_start(core0_sb[:], core0.rearrange("p r i -> r p i"))
         rows = held.tile([P, N], F32, name="rows", align_bytes=64)
-        nc.gpsimd.memset(rows[:], 0.0)
+        nc.vector.memset(rows[:], 0.0)
         for v, vector in enumerate((scale, bias)):
             nc.sync.dma_start(rows[v::B, :], vector.rearrange("o n -> (o n)").partition_broadcast(P // B))
         nc.sync.dma_start(windows[0][:], base[0:P, :])

@@ -25,13 +25,14 @@ def tile_tensorizedlinear_kernel(tc, x, core1, core0, scale, bias, base, offs, o
         tc.psum_pool(name="t_psum", bufs=TOKEN_BLOCKS * pieces) as t_psum,
         tc.psum_pool(name="y_psum", bufs=TOKEN_BLOCKS * M1) as y_psum,
     ):
-        x_sb = held.tile([P, N0, C], BF16, name="x_sb")
+        x_sb = [held.tile([P, C], BF16, name=f"x_sb{p}") for p in range(N0)]
         core1_sb = held.tile([P, M1, R], BF16, name="core1_sb")
         core0_sb = held.tile([P, N0, M0], BF16, name="core0_sb")
         offsets = held.tile([P, N // 16], U16, name="offsets")
         windows = [held.tile([P, S], F32, name=f"window{b}") for b in range(TOKEN_BLOCKS)]
 
-        nc.sync.dma_start(x_sb[:], x.rearrange("p k c -> k p c"))
+        for p in range(N0):
+            nc.sync.dma_start(x_sb[p][:], x[p])
         nc.scalar.dma_start(core1_sb[:], core1)
         nc.scalar.dma_start(core0_sb[:], core0.rearrange("p r i -> r p i"))
         rows = held.tile([P, N], F32, name="rows", align_bytes=64)
@@ -43,29 +44,28 @@ def tile_tensorizedlinear_kernel(tc, x, core1, core0, scale, bias, base, offs, o
         nc.sync.dma_start(windows[1][:], base[P : 2 * P, :])
 
         columns = held.tile([P, N], F32, name="columns", align_bytes=64)
-        nc.vector.transpose(columns[:], rows[:])
-        spread_rows = []
-        for v in range(2):
-            repeated = held.tile([P, N], F32, name=f"repeated{v}", align_bytes=64)
-            nc.vector.tensor_copy(
-                repeated[:].rearrange("p (b i) -> p b i", i=B),
-                columns[:].rearrange("p (b i) -> p b i", i=B)[:, :, v : v + 1].to_broadcast([P, N // B, B]),
-            )
-            spread = held.tile([P, N], F32, name=f"spread{v}", align_bytes=64)
-            nc.vector.transpose(spread[:], repeated[:])
-            spread_rows.append(spread)
-        scale_all, bias_all = spread_rows
+        repeated = [held.tile([P, N], F32, name=f"repeated{v}", align_bytes=64) for v in range(2)]
+        scale_all, bias_all = [held.tile([P, N], F32, name=f"spread{v}", align_bytes=64) for v in range(2)]
+        for m in range(M1):
+            features = slice(m * M0, (m + 1) * M0)
+            nc.vector.transpose(columns[:, features], rows[:, features])
+        for v, spread in enumerate((scale_all, bias_all)):
+            for m in range(M1):
+                features = slice(m * M0, (m + 1) * M0)
+                nc.vector.tensor_copy(
+                    repeated[v][:, features].rearrange("p (b i) -> p b i", i=B),
+                    columns[:, features].rearrange("p (b i) -> p b i", i=B)[:, :, v : v + 1].to_broadcast([P, M0 // B, B]),
+                )
+                nc.vector.transpose(spread[:, features], repeated[v][:, features])
 
         t_sb = {}
         for m in range(M1):
-            for b in range(TOKEN_BLOCKS):
-                t_ps = t_psum.tile([P, N0, P], BF16, name="t_ps")
-                nc.tensor.matmul(
-                    t_ps[:], core1_sb[:, m, :], x_sb[:, :, b * P : (b + 1) * P], start=True, stop=True
-                )
-                t_piece = t_pool.tile([P, N0, P], BF16, name="t_piece")
+            for p in range(N0):
+                t_ps = t_psum.tile([P, C], BF16, name="t_ps")
+                nc.tensor.matmul(t_ps[:], core1_sb[:, m, :], x_sb[p][:], start=True, stop=True)
+                t_piece = t_pool.tile([P, C], BF16, name="t_piece")
                 nc.scalar.copy(t_piece[:], t_ps[:])
-                t_sb[b, m] = t_piece
+                t_sb[p, m] = t_piece
 
         y_scaled = [y_pool.tile([P, N], F32, name=f"y_scaled{b}") for b in range(TOKEN_BLOCKS)]
         for m in range(M1):
@@ -74,7 +74,7 @@ def tile_tensorizedlinear_kernel(tc, x, core1, core0, scale, bias, base, offs, o
                 y_ps = y_psum.tile([P, M0], F32, name="y_ps")
                 for p in range(N0):
                     nc.tensor.matmul(
-                        y_ps[:], t_sb[b, m][:, p, :], core0_sb[:, p, :], start=(p == 0), stop=(p == N0 - 1)
+                        y_ps[:], t_sb[p, m][:, b * P : (b + 1) * P], core0_sb[:, p, :], start=(p == 0), stop=(p == N0 - 1)
                     )
                 nc.vector.scalar_tensor_tensor(
                     y_scaled[b][:, features], y_ps[:], ALPHA, scale_all[:, features], MULT, MULT

import concourse.mybir as mybir

BF16, F32, U16 = mybir.dt.bfloat16, mybir.dt.float32, mybir.dt.uint16
MULT, ADD = mybir.AluOpType.mult, mybir.AluOpType.add

P = 128
C, S, N = 256, 512, 256
N0, N1 = 2, 128
M1, M0 = 2, 128
R = 128
ALPHA = 1.5
TOKEN_BLOCKS = C // P
B = 32

FLOPS = 2 * (N0 * M1 * R * C) * N1 + 2 * (C * M1 * M0) * (N0 * R)


def tile_tensorizedlinear_kernel(tc, x, core1, core0, scale, bias, base, offs, out):
    nc = tc.nc
    pieces = M1
    with (
        tc.tile_pool(name="held", bufs=1) as held,
        tc.tile_pool(name="t_pool", bufs=TOKEN_BLOCKS * pieces) as t_pool,
        tc.tile_pool(name="y_pool", bufs=1) as y_pool,
        tc.psum_pool(name="t_psum", bufs=TOKEN_BLOCKS * pieces) as t_psum,
        tc.psum_pool(name="y_psum", bufs=TOKEN_BLOCKS * M1) as y_psum,
    ):
        x_sb = [held.tile([P, C], BF16, name=f"x_sb{p}") for p in range(N0)]
        core1_sb = held.tile([P, M1, R], BF16, name="core1_sb")
        core0_sb = held.tile([P, N0, M0], BF16, name="core0_sb")
        offsets = held.tile([P, N // 16], U16, name="offsets")
        windows = [held.tile([P, S], F32, name=f"window{b}") for b in range(TOKEN_BLOCKS)]

        for p in range(N0):
            nc.sync.dma_start(x_sb[p][:], x[p])
        nc.scalar.dma_start(core1_sb[:], core1)
        nc.scalar.dma_start(core0_sb[:], core0.rearrange("p r i -> r p i"))
        rows = held.tile([P, N], F32, name="rows", align_bytes=64)
        nc.vector.memset(rows[:], 0.0)
        for v, vector in enumerate((scale, bias)):
            nc.sync.dma_start(rows[v::B, :], vector.rearrange("o n -> (o n)").partition_broadcast(P // B))
        nc.sync.dma_start(windows[0][:], base[0:P, :])
        nc.sync.dma_start(offsets[:], offs)
        nc.sync.dma_start(windows[1][:], base[P : 2 * P, :])

        columns = held.tile([P, N], F32, name="columns", align_bytes=64)
        repeated = [held.tile([P, N], F32, name=f"repeated{v}", align_bytes=64) for v in range(2)]
        scale_all, bias_all = [held.tile([P, N], F32, name=f"spread{v}", align_bytes=64) for v in range(2)]
        for m in range(M1):
            features = slice(m * M0, (m + 1) * M0)
            nc.vector.transpose(columns[:, features], rows[:, features])
        for v, spread in enumerate((scale_all, bias_all)):
            for m in range(M1):
                features = slice(m * M0, (m + 1) * M0)
                nc.vector.tensor_copy(
                    repeated[v][:, features].rearrange("p (b i) -> p b i", i=B),
                    columns[:, features].rearrange("p (b i) -> p b i", i=B)[:, :, v : v + 1].to_broadcast([P, M0 // B, B]),
                )
                nc.vector.transpose(spread[:, features], repeated[v][:, features])

        t_sb = {}
        for m in range(M1):
            for p in range(N0):
                t_ps = t_psum.tile([P, C], BF16, name="t_ps")
                nc.tensor.matmul(t_ps[:], core1_sb[:, m, :], x_sb[p][:], start=True, stop=True)
                t_piece = t_pool.tile([P, C], BF16, name="t_piece")
                nc.scalar.copy(t_piece[:], t_ps[:])
                t_sb[p, m] = t_piece

        y_scaled = [y_pool.tile([P, N], F32, name=f"y_scaled{b}") for b in range(TOKEN_BLOCKS)]
        for m in range(M1):
            features = slice(m * M0, (m + 1) * M0)
            for b in range(TOKEN_BLOCKS):
                y_ps = y_psum.tile([P, M0], F32, name="y_ps")
                for p in range(N0):
                    nc.tensor.matmul(
                        y_ps[:], t_sb[p, m][:, b * P : (b + 1) * P], core0_sb[:, p, :], start=(p == 0), stop=(p == N0 - 1)
                    )
                nc.vector.scalar_tensor_tensor(
                    y_scaled[b][:, features], y_ps[:], ALPHA, scale_all[:, features], MULT, MULT
                )

        for b in range(TOKEN_BLOCKS):
            nc.vector.tensor_tensor(windows[b][:].indirect(offsets[:]), y_scaled[b][:], bias_all[:], ADD)
            nc.sync.dma_start(out[b * P : (b + 1) * P, :], windows[b][:])
